import numpy as np
import ml_dtypes

BF16 = ml_dtypes.bfloat16


def bf(x):
    return np.asarray(x, np.float32).astype(BF16)


def f32(x):
    return np.asarray(x, np.float32)


def f64(x):
    return np.asarray(x).astype(np.float64)


def striped(idx):
    return np.tile(idx.reshape(-1, 16).T, (8, 1))


C, S, N = 128, 4096, 1024
DEG = 6.0


def setup_inputs():
    et = (np.random.random((N, N)) < DEG / N).astype(np.float32)
    et = np.maximum(et, np.roll(np.eye(N, dtype=np.float32), 1, axis=0))
    d = np.arange(N)
    et[d, d] = (np.random.random(N) < 0.5).astype(np.float32)
    return {"base": f32(np.random.standard_normal((C, S))), "h": bf(1.5 * np.random.standard_normal((N, C))), "et": bf(et), "bias": f32(0.1 * np.random.standard_normal((C, 1))), "offs": striped(np.random.permutation(S)[:N])}


def reference(base, h, et, bias, offs):
    idx = offs[:16].T.reshape(-1)
    a = f64(et) + np.eye(N)
    a2 = a * a
    hh = f64(h)
    s = hh.T @ a
    q = (hh * hh).T @ a2
    den = a.sum(axis=0) ** 2 - a2.sum(axis=0)
    out = f64(base).copy()
    out[:, idx] = (s * s - q) * (1.0 / den)[None, :] + f64(bias)
    return out

@@ -1,0 +1,100 @@
+import concourse.mybir as mybir
+from concourse.masks import make_identity
+
+BF16, F32, U16 = mybir.dt.bfloat16, mybir.dt.float32, mybir.dt.uint16
+ADD, SUBTRACT, MULT = mybir.AluOpType.add, mybir.AluOpType.subtract, mybir.AluOpType.mult
+SQUARE, COPY = mybir.ActivationFunctionType.Square, mybir.ActivationFunctionType.Copy
+
+P = 128
+CHANNELS = 128
+SLOTS = 4096
+NODES = 1024
+BLOCKS = NODES // P
+WITH_ONES = CHANNELS + 1
+H_PITCH = CHANNELS + 16
+LOAD_COLS = 256
+LOADS = NODES // LOAD_COLS
+BLOCKS_A_LOAD = LOAD_COLS // P
+STORES = 4
+
+FLOPS = 2 * 2 * WITH_ONES * NODES * NODES
+
+
+def tile_bgnna_kernel(tc, base, h, et, bias, offs, out):
+    nc = tc.nc
+    with (
+        tc.tile_pool(name="held", bufs=1) as held,
+        tc.tile_pool(name="work", bufs=2) as work,
+        tc.psum_pool(name="psum", bufs=2) as psum,
+    ):
+        offsets = held.tile([P, NODES // 16], U16, name="offsets")
+        nc.sync.dma_start(offsets[:], offs)
+
+        h_ones = held.tile([P, BLOCKS, H_PITCH], BF16, name="h_ones")
+        nc.vector.memset(h_ones[:, :, CHANNELS:H_PITCH], 1.0)
+        nc.sync.dma_start(h_ones[:, :, 0:CHANNELS], h.rearrange("(kb p) c -> p kb c", p=P))
+
+        et_blocks = et.rearrange("(kb p) j -> p kb j", p=P)
+        a = [held.tile([P, BLOCKS, LOAD_COLS], BF16, name=f"a{g}") for g in range(LOADS)]
+        for g in range(LOADS):
+            nc.sync.dma_start(a[g][:], et_blocks[:, :, g * LOAD_COLS : (g + 1) * LOAD_COLS])
+
+        bias_col = held.tile([P, 1], F32, name="bias_col")
+        nc.sync.dma_start(bias_col[:], bias)
+        bias_wide = held.tile([P, NODES], F32, name="bias_wide")
+        nc.gpsimd.tensor_copy(bias_wide[:], bias_col[:, 0:1].to_broadcast([P, NODES]))
+        window = held.tile([P, SLOTS], F32, name="window")
+        nc.sync.dma_start(window[:], base)
+
+        identity_bf16 = held.tile([P, P], BF16, name="identity_bf16")
+        make_identity(nc, identity_bf16[:])
+        identity_f32 = held.tile([P, P], F32, name="identity_f32")
+        make_identity(nc, identity_f32[:])
+
+        h2_ones = held.tile([P, BLOCKS, H_PITCH], BF16, name="h2_ones")
+        nc.scalar.activation(h2_ones[:], h_ones[:], SQUARE)
+
+        a2 = [held.tile([P, BLOCKS, LOAD_COLS], BF16, name=f"a2_{g}") for g in range(LOADS)]
+        values = held.tile([P, NODES], F32, name="values")
+
+        for g in range(LOADS):
+            for r in range(BLOCKS_A_LOAD):
+                jb = g * BLOCKS_A_LOAD + r
+                diagonal = a[g][:, jb, r * P : (r + 1) * P]
+                nc.vector.tensor_tensor(diagonal, diagonal, identity_bf16[:], ADD)
+            half = BLOCKS // 2
+            nc.scalar.activation(a2[g][:, 0:half, :], a[g][:, 0:half, :], SQUARE)
+            nc.vector.tensor_tensor(a2[g][:, half:BLOCKS, :], a[g][:, half:BLOCKS, :], a[g][:, half:BLOCKS, :], MULT)
+
+            for r in range(BLOCKS_A_LOAD):
+                jb = g * BLOCKS_A_LOAD + r
+                cols = slice(r * P, (r + 1) * P)
+                s_t = psum.tile([P, WITH_ONES], F32, name="s_t")
+                for kb in range(BLOCKS):
+                    nc.tensor.matmul(s_t[:], a[g][:, kb, cols], h_ones[:, kb, 0:WITH_ONES],
+                                     start=(kb == 0), stop=(kb == BLOCKS - 1))
+                q_t = psum.tile([P, WITH_ONES], F32, name="q_t")
+                for kb in range(BLOCKS):
+                    nc.tensor.matmul(q_t[:], a2[g][:, kb, cols], h2_ones[:, kb, 0:WITH_ONES],
+                                     start=(kb == 0), stop=(kb == BLOCKS - 1))
+
+                s_squared = work.tile([P, WITH_ONES], F32, name="s_squared")
+                nc.scalar.activation(s_squared[:], s_t[:], SQUARE)
+                pairs = work.tile([P, WITH_ONES], F32, name="pairs")
+                nc.vector.tensor_tensor(pairs[:], s_squared[:], q_t[:], SUBTRACT)
+                one_over_den = work.tile([P, 1], F32, name="one_over_den")
+                nc.vector.reciprocal(one_over_den[:], pairs[:, CHANNELS:WITH_ONES])
+                scaled = work.tile([P, CHANNELS], F32, name="scaled")
+                nc.vector.tensor_scalar(scaled[:], pairs[:, 0:CHANNELS], one_over_den[:], None, MULT)
+
+                turned = psum.tile([P, P], F32, name="turned")
+                nc.tensor.transpose(turned[:], scaled[:], identity_f32[:])
+                nc.scalar.activation(values[:, jb * P : (jb + 1) * P], turned[:], COPY)
+
+        nc.vector.tensor_tensor(window[:].indirect(offsets[:]), values[:], bias_wide[:], ADD)
+
+        width = SLOTS // STORES
+        for piece in range(STORES):
+            queue = nc.sync if piece % 2 == 0 else nc.scalar
+            queue.dma_start(out[:, piece * width : (piece + 1) * width],
+                            window[:, piece * width : (piece + 1) * width])

@@ -24,7 +24,7 @@ def tile_bgnna_kernel(tc, base, h, et, bias, offs, out):
     nc = tc.nc
     with (
         tc.tile_pool(name="held", bufs=1) as held,
-        tc.tile_pool(name="work", bufs=2) as work,
+        tc.tile_pool(name="work", bufs=3) as work,
         tc.psum_pool(name="psum", bufs=2) as psum,
     ):
         offsets = held.tile([P, NODES // 16], U16, name="offsets")
@@ -52,12 +52,13 @@ def tile_bgnna_kernel(tc, base, h, et, bias, offs, out):
         make_identity(nc, identity_f32[:])
 
         h2_ones = held.tile([P, BLOCKS, H_PITCH], BF16, name="h2_ones")
-        nc.scalar.activation(h2_ones[:], h_ones[:], SQUARE)
+        nc.scalar.activation(h2_ones[:, :, CHANNELS:H_PITCH], h_ones[:, :, CHANNELS:H_PITCH], SQUARE)
+        nc.scalar.activation(h2_ones[:, :, 0:CHANNELS], h_ones[:, :, 0:CHANNELS], SQUARE)
 
         a2 = [held.tile([P, BLOCKS, LOAD_COLS], BF16, name=f"a2_{g}") for g in range(LOADS)]
         values = held.tile([P, NODES], F32, name="values")
 
-        for g in range(LOADS):
+        def prepare(g):
             for r in range(BLOCKS_A_LOAD):
                 jb = g * BLOCKS_A_LOAD + r
                 diagonal = a[g][:, jb, r * P : (r + 1) * P]
@@ -65,6 +66,12 @@ def tile_bgnna_kernel(tc, base, h, et, bias, offs, out):
             half = BLOCKS // 2
             nc.scalar.activation(a2[g][:, 0:half, :], a[g][:, 0:half, :], SQUARE)
             nc.vector.tensor_tensor(a2[g][:, half:BLOCKS, :], a[g][:, half:BLOCKS, :], a[g][:, half:BLOCKS, :], MULT)
+
+        waiting = []
+        prepare(0)
+        for g in range(LOADS):
+            if g + 1 < LOADS:
+                prepare(g + 1)
 
             for r in range(BLOCKS_A_LOAD):
                 jb = g * BLOCKS_A_LOAD + r
@@ -87,9 +94,13 @@ def tile_bgnna_kernel(tc, base, h, et, bias, offs, out):
                 scaled = work.tile([P, CHANNELS], F32, name="scaled")
                 nc.vector.tensor_scalar(scaled[:], pairs[:, 0:CHANNELS], one_over_den[:], None, MULT)
 
-                turned = psum.tile([P, P], F32, name="turned")
-                nc.tensor.transpose(turned[:], scaled[:], identity_f32[:])
-                nc.scalar.activation(values[:, jb * P : (jb + 1) * P], turned[:], COPY)
+                waiting.append((jb, scaled))
+
+                while len(waiting) > (1 if jb < BLOCKS - 1 else 0):
+                    turn_jb, turn_scaled = waiting.pop(0)
+                    turned = psum.tile([P, P], F32, name="turned")
+                    nc.tensor.transpose(turned[:], turn_scaled[:], identity_f32[:])
+                    nc.scalar.activation(values[:, turn_jb * P : (turn_jb + 1) * P], turned[:], COPY)
 
         nc.vector.tensor_tensor(window[:].indirect(offsets[:]), values[:], bias_wide[:], ADD)
 

@@ -15,6 +15,7 @@ H_PITCH = CHANNELS + 16
 LOAD_COLS = 256
 LOADS = NODES // LOAD_COLS
 BLOCKS_A_LOAD = LOAD_COLS // P
+WARM_UP = 24
 STORES = 4
 
 FLOPS = 2 * 2 * WITH_ONES * NODES * NODES
@@ -24,23 +25,23 @@ def tile_bgnna_kernel(tc, base, h, et, bias, offs, out):
     nc = tc.nc
     with (
         tc.tile_pool(name="held", bufs=1) as held,
+        tc.tile_pool(name="squares", bufs=2) as squares,
         tc.tile_pool(name="work", bufs=3) as work,
         tc.psum_pool(name="psum", bufs=2) as psum,
     ):
-        offsets = held.tile([P, NODES // 16], U16, name="offsets")
-        nc.sync.dma_start(offsets[:], offs)
-
         h_ones = held.tile([P, BLOCKS, H_PITCH], BF16, name="h_ones")
         nc.vector.memset(h_ones[:, :, CHANNELS:H_PITCH], 1.0)
-        nc.sync.dma_start(h_ones[:, :, 0:CHANNELS], h.rearrange("(kb p) c -> p kb c", p=P))
+        nc.scalar.dma_start(h_ones[:, :, 0:CHANNELS], h.rearrange("(kb p) c -> p kb c", p=P))
 
         et_blocks = et.rearrange("(kb p) j -> p kb j", p=P)
         a = [held.tile([P, BLOCKS, LOAD_COLS], BF16, name=f"a{g}") for g in range(LOADS)]
         for g in range(LOADS):
             nc.sync.dma_start(a[g][:], et_blocks[:, :, g * LOAD_COLS : (g + 1) * LOAD_COLS])
 
+        offsets = held.tile([P, NODES // 16], U16, name="offsets")
+        nc.sync.dma_start(offsets[:], offs)
         bias_col = held.tile([P, 1], F32, name="bias_col")
-        nc.sync.dma_start(bias_col[:], bias)
+        nc.scalar.dma_start(bias_col[:], bias)
         bias_wide = held.tile([P, NODES], F32, name="bias_wide")
         nc.gpsimd.tensor_copy(bias_wide[:], bias_col[:, 0:1].to_broadcast([P, NODES]))
         window = held.tile([P, SLOTS], F32, name="window")
@@ -51,11 +52,15 @@ def tile_bgnna_kernel(tc, base, h, et, bias, offs, out):
         identity_f32 = held.tile([P, P], F32, name="identity_f32")
         make_identity(nc, identity_f32[:])
 
+        warm = psum.tile([P, P], F32, name="warm", bufs=1)
+        for i in range(WARM_UP):
+            nc.tensor.matmul(warm[:], identity_bf16[:], identity_bf16[:], start=True, stop=True)
+
         h2_ones = held.tile([P, BLOCKS, H_PITCH], BF16, name="h2_ones")
         nc.scalar.activation(h2_ones[:, :, CHANNELS:H_PITCH], h_ones[:, :, CHANNELS:H_PITCH], SQUARE)
         nc.scalar.activation(h2_ones[:, :, 0:CHANNELS], h_ones[:, :, 0:CHANNELS], SQUARE)
 
-        a2 = [held.tile([P, BLOCKS, LOAD_COLS], BF16, name=f"a2_{g}") for g in range(LOADS)]
+        a2 = {}
         values = held.tile([P, NODES], F32, name="values")
 
         def prepare(g):
@@ -63,6 +68,7 @@ def tile_bgnna_kernel(tc, base, h, et, bias, offs, out):
                 jb = g * BLOCKS_A_LOAD + r
                 diagonal = a[g][:, jb, r * P : (r + 1) * P]
                 nc.vector.tensor_tensor(diagonal, diagonal, identity_bf16[:], ADD)
+            a2[g] = squares.tile([P, BLOCKS, LOAD_COLS], BF16, name="a2")
             half = BLOCKS // 2
             nc.scalar.activation(a2[g][:, 0:half, :], a[g][:, 0:half, :], SQUARE)
             nc.vector.tensor_tensor(a2[g][:, half:BLOCKS, :], a[g][:, half:BLOCKS, :], a[g][:, half:BLOCKS, :], MULT)
@@ -76,14 +82,15 @@ def tile_bgnna_kernel(tc, base, h, et, bias, offs, out):
             for r in range(BLOCKS_A_LOAD):
                 jb = g * BLOCKS_A_LOAD + r
                 cols = slice(r * P, (r + 1) * P)
+                row_blocks = [(jb + 1 + i) % BLOCKS for i in range(BLOCKS)]
                 s_t = psum.tile([P, WITH_ONES], F32, name="s_t")
-                for kb in range(BLOCKS):
+                for kb in row_blocks:
                     nc.tensor.matmul(s_t[:], a[g][:, kb, cols], h_ones[:, kb, 0:WITH_ONES],
-                                     start=(kb == 0), stop=(kb == BLOCKS - 1))
+                                     start=(kb == row_blocks[0]), stop=(kb == jb))
                 q_t = psum.tile([P, WITH_ONES], F32, name="q_t")
-                for kb in range(BLOCKS):
+                for kb in row_blocks:
                     nc.tensor.matmul(q_t[:], a2[g][:, kb, cols], h2_ones[:, kb, 0:WITH_ONES],
-                                     start=(kb == 0), stop=(kb == BLOCKS - 1))
+                                     start=(kb == row_blocks[0]), stop=(kb == jb))
 
                 s_squared = work.tile([P, WITH_ONES], F32, name="s_squared")
                 nc.scalar.activation(s_squared[:], s_t[:], SQUARE)

@@ -15,7 +15,6 @@ H_PITCH = CHANNELS + 16
 LOAD_COLS = 256
 LOADS = NODES // LOAD_COLS
 BLOCKS_A_LOAD = LOAD_COLS // P
-WARM_UP = 24
 STORES = 4
 
 FLOPS = 2 * 2 * WITH_ONES * NODES * NODES
@@ -51,10 +50,6 @@ def tile_bgnna_kernel(tc, base, h, et, bias, offs, out):
         make_identity(nc, identity_bf16[:])
         identity_f32 = held.tile([P, P], F32, name="identity_f32")
         make_identity(nc, identity_f32[:])
-
-        warm = psum.tile([P, P], F32, name="warm", bufs=1)
-        for i in range(WARM_UP):
-            nc.tensor.matmul(warm[:], identity_bf16[:], identity_bf16[:], start=True, stop=True)
 
         h2_ones = held.tile([P, BLOCKS, H_PITCH], BF16, name="h2_ones")
         nc.scalar.activation(h2_ones[:, :, CHANNELS:H_PITCH], h_ones[:, :, CHANNELS:H_PITCH], SQUARE)

@@ -15,6 +15,7 @@ H_PITCH = CHANNELS + 16
 LOAD_COLS = 256
 LOADS = NODES // LOAD_COLS
 BLOCKS_A_LOAD = LOAD_COLS // P
+TURN_BEHIND = 2
 STORES = 4
 
 FLOPS = 2 * 2 * WITH_ONES * NODES * NODES
@@ -25,7 +26,7 @@ def tile_bgnna_kernel(tc, base, h, et, bias, offs, out):
     with (
         tc.tile_pool(name="held", bufs=1) as held,
         tc.tile_pool(name="squares", bufs=2) as squares,
-        tc.tile_pool(name="work", bufs=3) as work,
+        tc.tile_pool(name="work", bufs=4) as work,
         tc.psum_pool(name="psum", bufs=2) as psum,
     ):
         h_ones = held.tile([P, BLOCKS, H_PITCH], BF16, name="h_ones")
@@ -98,7 +99,7 @@ def tile_bgnna_kernel(tc, base, h, et, bias, offs, out):
 
                 waiting.append((jb, scaled))
 
-                while len(waiting) > (1 if jb < BLOCKS - 1 else 0):
+                while len(waiting) > (TURN_BEHIND if jb < BLOCKS - 1 else 0):
                     turn_jb, turn_scaled = waiting.pop(0)
                     turned = psum.tile([P, P], F32, name="turned")
                     nc.tensor.transpose(turned[:], turn_scaled[:], identity_f32[:])

@@ -15,7 +15,7 @@ H_PITCH = CHANNELS + 16
 LOAD_COLS = 256
 LOADS = NODES // LOAD_COLS
 BLOCKS_A_LOAD = LOAD_COLS // P
-TURN_BEHIND = 2
+TURN_BEHIND = 3
 STORES = 4
 
 FLOPS = 2 * 2 * WITH_ONES * NODES * NODES
@@ -26,7 +26,7 @@ def tile_bgnna_kernel(tc, base, h, et, bias, offs, out):
     with (
         tc.tile_pool(name="held", bufs=1) as held,
         tc.tile_pool(name="squares", bufs=2) as squares,
-        tc.tile_pool(name="work", bufs=4) as work,
+        tc.tile_pool(name="work", bufs=5) as work,
         tc.psum_pool(name="psum", bufs=2) as psum,
     ):
         h_ones = held.tile([P, BLOCKS, H_PITCH], BF16, name="h_ones")
@@ -79,11 +79,11 @@ def tile_bgnna_kernel(tc, base, h, et, bias, offs, out):
                 jb = g * BLOCKS_A_LOAD + r
                 cols = slice(r * P, (r + 1) * P)
                 row_blocks = [(jb + 1 + i) % BLOCKS for i in range(BLOCKS)]
-                s_t = psum.tile([P, WITH_ONES], F32, name="s_t")
+                s_t = psum.tile([P, WITH_ONES], F32, name="s_t", bufs=3)
                 for kb in row_blocks:
                     nc.tensor.matmul(s_t[:], a[g][:, kb, cols], h_ones[:, kb, 0:WITH_ONES],
                                      start=(kb == row_blocks[0]), stop=(kb == jb))
-                q_t = psum.tile([P, WITH_ONES], F32, name="q_t")
+                q_t = psum.tile([P, WITH_ONES], F32, name="q_t", bufs=3)
                 for kb in row_blocks:
                     nc.tensor.matmul(q_t[:], a2[g][:, kb, cols], h2_ones[:, kb, 0:WITH_ONES],
                                      start=(kb == row_blocks[0]), stop=(kb == jb))

@@ -10,38 +10,45 @@ CHANNELS = 128
 SLOTS = 4096
 NODES = 1024
 BLOCKS = NODES // P
-WITH_ONES = CHANNELS + 1
-H_PITCH = CHANNELS + 16
-LOAD_COLS = 256
-LOADS = NODES // LOAD_COLS
-BLOCKS_A_LOAD = LOAD_COLS // P
+WITH_ONE = 1 + CHANNELS
+H_FROM = 16
+ONE_FROM = H_FROM - 1
+H2_FROM = H_FROM + CHANNELS
+H_PITCH = H2_FROM + WITH_ONE + 15
+TILE_COLS = 256
+TILES = NODES // TILE_COLS
+BLOCKS_A_TILE = TILE_COLS // P
+HALF = BLOCKS // 2
+AHEAD = 2
 TURN_BEHIND = 3
 STORES = 4
 
-FLOPS = 2 * 2 * WITH_ONES * NODES * NODES
+FLOPS = 2 * 2 * WITH_ONE * NODES * NODES
 
 
 def tile_bgnna_kernel(tc, base, h, et, bias, offs, out):
     nc = tc.nc
     with (
         tc.tile_pool(name="held", bufs=1) as held,
-        tc.tile_pool(name="squares", bufs=2) as squares,
         tc.tile_pool(name="work", bufs=5) as work,
         tc.psum_pool(name="psum", bufs=2) as psum,
     ):
-        h_ones = held.tile([P, BLOCKS, H_PITCH], BF16, name="h_ones")
-        nc.vector.memset(h_ones[:, :, CHANNELS:H_PITCH], 1.0)
-        nc.scalar.dma_start(h_ones[:, :, 0:CHANNELS], h.rearrange("(kb p) c -> p kb c", p=P))
+        moving = held.tile([P, BLOCKS, H_PITCH], BF16, name="moving")
+        nc.vector.memset(moving[:, :, 0:H_FROM], 1.0)
+        h_blocks = h.rearrange("(kb p) c -> p kb c", p=P)
+        for rows in (slice(0, HALF), slice(HALF, BLOCKS)):
+            nc.scalar.dma_start(moving[:, rows, H_FROM:H2_FROM], h_blocks[:, rows, :])
 
         et_blocks = et.rearrange("(kb p) j -> p kb j", p=P)
-        a = [held.tile([P, BLOCKS, LOAD_COLS], BF16, name=f"a{g}") for g in range(LOADS)]
-        for g in range(LOADS):
-            nc.sync.dma_start(a[g][:], et_blocks[:, :, g * LOAD_COLS : (g + 1) * LOAD_COLS])
+        a = [held.tile([P, BLOCKS, TILE_COLS], BF16, name=f"a{g}") for g in range(TILES)]
+        for g in range(TILES):
+            for rows in (slice(0, HALF), slice(HALF, BLOCKS)):
+                nc.sync.dma_start(a[g][:, rows, :], et_blocks[:, rows, g * TILE_COLS : (g + 1) * TILE_COLS])
 
         offsets = held.tile([P, NODES // 16], U16, name="offsets")
         nc.sync.dma_start(offsets[:], offs)
         bias_col = held.tile([P, 1], F32, name="bias_col")
-        nc.scalar.dma_start(bias_col[:], bias)
+        nc.gpsimd.dma_start(bias_col[:], bias)
         bias_wide = held.tile([P, NODES], F32, name="bias_wide")
         nc.gpsimd.tensor_copy(bias_wide[:], bias_col[:, 0:1].to_broadcast([P, NODES]))
         window = held.tile([P, SLOTS], F32, name="window")
@@ -52,58 +59,56 @@ def tile_bgnna_kernel(tc, base, h, et, bias, offs, out):
         identity_f32 = held.tile([P, P], F32, name="identity_f32")
         make_identity(nc, identity_f32[:])
 
-        h2_ones = held.tile([P, BLOCKS, H_PITCH], BF16, name="h2_ones")
-        nc.scalar.activation(h2_ones[:, :, CHANNELS:H_PITCH], h_ones[:, :, CHANNELS:H_PITCH], SQUARE)
-        nc.scalar.activation(h2_ones[:, :, 0:CHANNELS], h_ones[:, :, 0:CHANNELS], SQUARE)
+        nc.scalar.activation(moving[:, HALF:BLOCKS, H2_FROM : H2_FROM + 1], moving[:, HALF:BLOCKS, ONE_FROM:H_FROM], SQUARE)
+        nc.vector.tensor_tensor(moving[:, 0:HALF, H2_FROM : H2_FROM + WITH_ONE], moving[:, 0:HALF, ONE_FROM:H2_FROM],
+                                moving[:, 0:HALF, ONE_FROM:H2_FROM], MULT)
+        nc.scalar.activation(moving[:, HALF:BLOCKS, H2_FROM + 1 : H2_FROM + WITH_ONE], moving[:, HALF:BLOCKS, H_FROM:H2_FROM], SQUARE)
 
-        a2 = {}
+        diagonal = held.tile([P, BLOCKS, P], BF16, name="diagonal")
+        diagonal_squared = held.tile([P, BLOCKS, P], BF16, name="diagonal_squared")
         values = held.tile([P, NODES], F32, name="values")
 
-        def prepare(g):
-            for r in range(BLOCKS_A_LOAD):
-                jb = g * BLOCKS_A_LOAD + r
-                diagonal = a[g][:, jb, r * P : (r + 1) * P]
-                nc.vector.tensor_tensor(diagonal, diagonal, identity_bf16[:], ADD)
-            a2[g] = squares.tile([P, BLOCKS, LOAD_COLS], BF16, name="a2")
-            half = BLOCKS // 2
-            nc.scalar.activation(a2[g][:, 0:half, :], a[g][:, 0:half, :], SQUARE)
-            nc.vector.tensor_tensor(a2[g][:, half:BLOCKS, :], a[g][:, half:BLOCKS, :], a[g][:, half:BLOCKS, :], MULT)
+        def a_block(kb, jb):
+            g, r = divmod(jb, BLOCKS_A_TILE)
+            return a[g][:, kb, r * P : (r + 1) * P]
+
+        def prepare(jb):
+            nc.vector.tensor_tensor(diagonal[:, jb, :], a_block(jb, jb), identity_bf16[:], ADD)
+            nc.scalar.activation(diagonal_squared[:, jb, :], diagonal[:, jb, :], SQUARE)
 
         waiting = []
-        prepare(0)
-        for g in range(LOADS):
-            if g + 1 < LOADS:
-                prepare(g + 1)
+        for jb in range(AHEAD):
+            prepare(jb)
+        for jb in range(BLOCKS):
+            if jb + AHEAD < BLOCKS:
+                prepare(jb + AHEAD)
 
-            for r in range(BLOCKS_A_LOAD):
-                jb = g * BLOCKS_A_LOAD + r
-                cols = slice(r * P, (r + 1) * P)
-                row_blocks = [(jb + 1 + i) % BLOCKS for i in range(BLOCKS)]
-                s_t = psum.tile([P, WITH_ONES], F32, name="s_t", bufs=3)
-                for kb in row_blocks:
-                    nc.tensor.matmul(s_t[:], a[g][:, kb, cols], h_ones[:, kb, 0:WITH_ONES],
-                                     start=(kb == row_blocks[0]), stop=(kb == jb))
-                q_t = psum.tile([P, WITH_ONES], F32, name="q_t", bufs=3)
-                for kb in row_blocks:
-                    nc.tensor.matmul(q_t[:], a2[g][:, kb, cols], h2_ones[:, kb, 0:WITH_ONES],
-                                     start=(kb == row_blocks[0]), stop=(kb == jb))
+            sq_t = psum.tile([P, 2 * WITH_ONE], F32, name="sq_t", bufs=5)
+            others = [(jb + 1 + i) % BLOCKS for i in range(BLOCKS - 1)]
+            for kb in others:
+                nc.tensor.matmul(sq_t[:], a_block(kb, jb), moving[:, kb, ONE_FROM : H2_FROM + WITH_ONE],
+                                 start=(kb == others[0]), stop=False)
+            nc.tensor.matmul(sq_t[:, 0:WITH_ONE], diagonal[:, jb, :], moving[:, jb, ONE_FROM:H2_FROM],
+                             start=False, stop=False)
+            nc.tensor.matmul(sq_t[:, WITH_ONE : 2 * WITH_ONE], diagonal_squared[:, jb, :],
+                             moving[:, jb, H2_FROM : H2_FROM + WITH_ONE], start=False, stop=True)
 
-                s_squared = work.tile([P, WITH_ONES], F32, name="s_squared")
-                nc.scalar.activation(s_squared[:], s_t[:], SQUARE)
-                pairs = work.tile([P, WITH_ONES], F32, name="pairs")
-                nc.vector.tensor_tensor(pairs[:], s_squared[:], q_t[:], SUBTRACT)
-                one_over_den = work.tile([P, 1], F32, name="one_over_den")
-                nc.vector.reciprocal(one_over_den[:], pairs[:, CHANNELS:WITH_ONES])
-                scaled = work.tile([P, CHANNELS], F32, name="scaled")
-                nc.vector.tensor_scalar(scaled[:], pairs[:, 0:CHANNELS], one_over_den[:], None, MULT)
+            s_squared = work.tile([P, WITH_ONE], F32, name="s_squared")
+            nc.scalar.activation(s_squared[:], sq_t[:, 0:WITH_ONE], SQUARE)
+            pairs = work.tile([P, WITH_ONE], F32, name="pairs")
+            nc.vector.tensor_tensor(pairs[:], s_squared[:], sq_t[:, WITH_ONE : 2 * WITH_ONE], SUBTRACT)
+            one_over_den = work.tile([P, 1], F32, name="one_over_den")
+            nc.vector.reciprocal(one_over_den[:], pairs[:, 0:1])
+            scaled = work.tile([P, CHANNELS], F32, name="scaled")
+            nc.vector.tensor_scalar(scaled[:], pairs[:, 1:WITH_ONE], one_over_den[:], None, MULT)
 
-                waiting.append((jb, scaled))
+            waiting.append((jb, scaled))
 
-                while len(waiting) > (TURN_BEHIND if jb < BLOCKS - 1 else 0):
-                    turn_jb, turn_scaled = waiting.pop(0)
-                    turned = psum.tile([P, P], F32, name="turned")
-                    nc.tensor.transpose(turned[:], turn_scaled[:], identity_f32[:])
-                    nc.scalar.activation(values[:, turn_jb * P : (turn_jb + 1) * P], turned[:], COPY)
+            while len(waiting) > (TURN_BEHIND if jb < BLOCKS - 1 else 0):
+                turn_jb, turn_scaled = waiting.pop(0)
+                turned = psum.tile([P, P], F32, name="turned", bufs=3)
+                nc.tensor.transpose(turned[:], turn_scaled[:], identity_f32[:])
+                nc.scalar.activation(values[:, turn_jb * P : (turn_jb + 1) * P], turned[:], COPY)
 
         nc.vector.tensor_tensor(window[:].indirect(offsets[:]), values[:], bias_wide[:], ADD)
 

@@ -20,7 +20,7 @@ TILES = NODES // TILE_COLS
 BLOCKS_A_TILE = TILE_COLS // P
 HALF = BLOCKS // 2
 AHEAD = 2
-TURN_BEHIND = 3
+TURN_GROUPS = ((0, 1, 2, 3), (4, 5, 6), (7,))
 STORES = 4
 
 FLOPS = 2 * 2 * WITH_ONE * NODES * NODES
@@ -76,7 +76,7 @@ def tile_bgnna_kernel(tc, base, h, et, bias, offs, out):
             nc.vector.tensor_tensor(diagonal[:, jb, :], a_block(jb, jb), identity_bf16[:], ADD)
             nc.scalar.activation(diagonal_squared[:, jb, :], diagonal[:, jb, :], SQUARE)
 
-        waiting = []
+        scaled_blocks = []
         for jb in range(AHEAD):
             prepare(jb)
         for jb in range(BLOCKS):
@@ -99,16 +99,20 @@ def tile_bgnna_kernel(tc, base, h, et, bias, offs, out):
             nc.vector.tensor_tensor(pairs[:], s_squared[:], sq_t[:, WITH_ONE : 2 * WITH_ONE], SUBTRACT)
             one_over_den = work.tile([P, 1], F32, name="one_over_den")
             nc.vector.reciprocal(one_over_den[:], pairs[:, 0:1])
-            scaled = work.tile([P, CHANNELS], F32, name="scaled")
+            scaled = work.tile([P, CHANNELS], F32, name="scaled", bufs=BLOCKS)
             nc.vector.tensor_scalar(scaled[:], pairs[:, 1:WITH_ONE], one_over_den[:], None, MULT)
 
-            waiting.append((jb, scaled))
+            scaled_blocks.append(scaled)
 
-            while len(waiting) > (TURN_BEHIND if jb < BLOCKS - 1 else 0):
-                turn_jb, turn_scaled = waiting.pop(0)
-                turned = psum.tile([P, P], F32, name="turned", bufs=3)
-                nc.tensor.transpose(turned[:], turn_scaled[:], identity_f32[:])
-                nc.scalar.activation(values[:, turn_jb * P : (turn_jb + 1) * P], turned[:], COPY)
+        for group in TURN_GROUPS:
+            turned = psum.tile([P, len(group) * P], F32, name="turned", bufs=len(TURN_GROUPS))
+            for i, jb in enumerate(group):
+                nc.tensor.transpose(turned[:, i * P : (i + 1) * P], scaled_blocks[jb][:], identity_f32[:])
+            group_values = values[:, group[0] * P : (group[-1] + 1) * P]
+            if group == TURN_GROUPS[1]:
+                nc.vector.tensor_copy(group_values, turned[:])
+            else:
+                nc.scalar.activation(group_values, turned[:], COPY)
 
         nc.vector.tensor_tensor(window[:].indirect(offsets[:]), values[:], bias_wide[:], ADD)
 

@@ -10,11 +10,10 @@ CHANNELS = 128
 SLOTS = 4096
 NODES = 1024
 BLOCKS = NODES // P
-WITH_ONE = 1 + CHANNELS
-H_FROM = 16
-ONE_FROM = H_FROM - 1
-H2_FROM = H_FROM + CHANNELS
-H_PITCH = H2_FROM + WITH_ONE + 15
+WITH_ONE = CHANNELS + 1
+H2_FROM = WITH_ONE + 1
+MOVING_COLS = H2_FROM + WITH_ONE
+MOVING_PITCH = MOVING_COLS + 13
 TILE_COLS = 256
 TILES = NODES // TILE_COLS
 BLOCKS_A_TILE = TILE_COLS // P
@@ -33,17 +32,16 @@ def tile_bgnna_kernel(tc, base, h, et, bias, offs, out):
         tc.tile_pool(name="work", bufs=5) as work,
         tc.psum_pool(name="psum", bufs=2) as psum,
     ):
-        moving = held.tile([P, BLOCKS, H_PITCH], BF16, name="moving")
-        nc.vector.memset(moving[:, :, 0:H_FROM], 1.0)
-        h_blocks = h.rearrange("(kb p) c -> p kb c", p=P)
-        for rows in (slice(0, HALF), slice(HALF, BLOCKS)):
-            nc.scalar.dma_start(moving[:, rows, H_FROM:H2_FROM], h_blocks[:, rows, :])
+        moving = held.tile([P, BLOCKS, MOVING_PITCH], BF16, name="moving")
+        nc.vector.memset(moving[:, :, CHANNELS:H2_FROM], 1.0)
+        nc.sync.dma_start(moving[:, :, 0:CHANNELS], h.rearrange("(kb p) c -> p kb c", p=P))
 
         et_blocks = et.rearrange("(kb p) j -> p kb j", p=P)
         a = [held.tile([P, BLOCKS, TILE_COLS], BF16, name=f"a{g}") for g in range(TILES)]
         for g in range(TILES):
             for rows in (slice(0, HALF), slice(HALF, BLOCKS)):
-                nc.sync.dma_start(a[g][:, rows, :], et_blocks[:, rows, g * TILE_COLS : (g + 1) * TILE_COLS])
+                queue = nc.scalar if (g == 0 and rows.start == 0) else nc.sync
+                queue.dma_start(a[g][:, rows, :], et_blocks[:, rows, g * TILE_COLS : (g + 1) * TILE_COLS])
 
         offsets = held.tile([P, NODES // 16], U16, name="offsets")
         nc.sync.dma_start(offsets[:], offs)
@@ -59,10 +57,10 @@ def tile_bgnna_kernel(tc, base, h, et, bias, offs, out):
         identity_f32 = held.tile([P, P], F32, name="identity_f32")
         make_identity(nc, identity_f32[:])
 
-        nc.scalar.activation(moving[:, HALF:BLOCKS, H2_FROM : H2_FROM + 1], moving[:, HALF:BLOCKS, ONE_FROM:H_FROM], SQUARE)
-        nc.vector.tensor_tensor(moving[:, 0:HALF, H2_FROM : H2_FROM + WITH_ONE], moving[:, 0:HALF, ONE_FROM:H2_FROM],
-                                moving[:, 0:HALF, ONE_FROM:H2_FROM], MULT)
-        nc.scalar.activation(moving[:, HALF:BLOCKS, H2_FROM + 1 : H2_FROM + WITH_ONE], moving[:, HALF:BLOCKS, H_FROM:H2_FROM], SQUARE)
+        nc.scalar.activation(moving[:, :, MOVING_COLS - 1 : MOVING_COLS + 1], moving[:, :, CHANNELS:H2_FROM], SQUARE)
+        nc.vector.tensor_tensor(moving[:, 0:HALF, H2_FROM : H2_FROM + CHANNELS], moving[:, 0:HALF, 0:CHANNELS],
+                                moving[:, 0:HALF, 0:CHANNELS], MULT)
+        nc.scalar.activation(moving[:, HALF:BLOCKS, H2_FROM : H2_FROM + CHANNELS], moving[:, HALF:BLOCKS, 0:CHANNELS], SQUARE)
 
         diagonal = held.tile([P, BLOCKS, P], BF16, name="diagonal")
         diagonal_squared = held.tile([P, BLOCKS, P], BF16, name="diagonal_squared")
@@ -83,25 +81,24 @@ def tile_bgnna_kernel(tc, base, h, et, bias, offs, out):
             if jb + AHEAD < BLOCKS:
                 prepare(jb + AHEAD)
 
-            sq_t = psum.tile([P, 2 * WITH_ONE], F32, name="sq_t", bufs=5)
+            sq_t = psum.tile([P, MOVING_COLS], F32, name="sq_t", bufs=5)
             others = [(jb + 1 + i) % BLOCKS for i in range(BLOCKS - 1)]
             for kb in others:
-                nc.tensor.matmul(sq_t[:], a_block(kb, jb), moving[:, kb, ONE_FROM : H2_FROM + WITH_ONE],
+                nc.tensor.matmul(sq_t[:], a_block(kb, jb), moving[:, kb, 0:MOVING_COLS],
                                  start=(kb == others[0]), stop=False)
-            nc.tensor.matmul(sq_t[:, 0:WITH_ONE], diagonal[:, jb, :], moving[:, jb, ONE_FROM:H2_FROM],
+            nc.tensor.matmul(sq_t[:, 0:H2_FROM], diagonal[:, jb, :], moving[:, jb, 0:H2_FROM],
                              start=False, stop=False)
-            nc.tensor.matmul(sq_t[:, WITH_ONE : 2 * WITH_ONE], diagonal_squared[:, jb, :],
-                             moving[:, jb, H2_FROM : H2_FROM + WITH_ONE], start=False, stop=True)
+            nc.tensor.matmul(sq_t[:, H2_FROM:MOVING_COLS], diagonal_squared[:, jb, :],
+                             moving[:, jb, H2_FROM:MOVING_COLS], start=False, stop=True)
 
             s_squared = work.tile([P, WITH_ONE], F32, name="s_squared")
             nc.scalar.activation(s_squared[:], sq_t[:, 0:WITH_ONE], SQUARE)
             pairs = work.tile([P, WITH_ONE], F32, name="pairs")
-            nc.vector.tensor_tensor(pairs[:], s_squared[:], sq_t[:, WITH_ONE : 2 * WITH_ONE], SUBTRACT)
+            nc.vector.tensor_tensor(pairs[:], s_squared[:], sq_t[:, H2_FROM:MOVING_COLS], SUBTRACT)
             one_over_den = work.tile([P, 1], F32, name="one_over_den")
-            nc.vector.reciprocal(one_over_den[:], pairs[:, 0:1])
+            nc.vector.reciprocal(one_over_den[:], pairs[:, CHANNELS:WITH_ONE])
             scaled = work.tile([P, CHANNELS], F32, name="scaled", bufs=BLOCKS)
-            nc.vector.tensor_scalar(scaled[:], pairs[:, 1:WITH_ONE], one_over_den[:], None, MULT)
-
+            nc.vector.tensor_scalar(scaled[:], pairs[:, 0:CHANNELS], one_over_den[:], None, MULT)
             scaled_blocks.append(scaled)
 
         for group in TURN_GROUPS:

@@ -12,8 +12,8 @@ NODES = 1024
 BLOCKS = NODES // P
 WITH_ONE = CHANNELS + 1
 H2_FROM = WITH_ONE + 1
-MOVING_COLS = H2_FROM + WITH_ONE
-MOVING_PITCH = MOVING_COLS + 13
+MOVING_COLS = 2 * H2_FROM
+MOVING_PITCH = MOVING_COLS + 28
 TILE_COLS = 256
 TILES = NODES // TILE_COLS
 BLOCKS_A_TILE = TILE_COLS // P
@@ -57,7 +57,7 @@ def tile_bgnna_kernel(tc, base, h, et, bias, offs, out):
         identity_f32 = held.tile([P, P], F32, name="identity_f32")
         make_identity(nc, identity_f32[:])
 
-        nc.scalar.activation(moving[:, :, MOVING_COLS - 1 : MOVING_COLS + 1], moving[:, :, CHANNELS:H2_FROM], SQUARE)
+        nc.scalar.activation(moving[:, :, MOVING_COLS - 2 : MOVING_COLS], moving[:, :, CHANNELS:H2_FROM], SQUARE)
         nc.vector.tensor_tensor(moving[:, 0:HALF, H2_FROM : H2_FROM + CHANNELS], moving[:, 0:HALF, 0:CHANNELS],
                                 moving[:, 0:HALF, 0:CHANNELS], MULT)
         nc.scalar.activation(moving[:, HALF:BLOCKS, H2_FROM : H2_FROM + CHANNELS], moving[:, HALF:BLOCKS, 0:CHANNELS], SQUARE)
@@ -94,7 +94,7 @@ def tile_bgnna_kernel(tc, base, h, et, bias, offs, out):
             s_squared = work.tile([P, WITH_ONE], F32, name="s_squared")
             nc.scalar.activation(s_squared[:], sq_t[:, 0:WITH_ONE], SQUARE)
             pairs = work.tile([P, WITH_ONE], F32, name="pairs")
-            nc.vector.tensor_tensor(pairs[:], s_squared[:], sq_t[:, H2_FROM:MOVING_COLS], SUBTRACT)
+            nc.vector.tensor_tensor(pairs[:], s_squared[:], sq_t[:, H2_FROM : H2_FROM + WITH_ONE], SUBTRACT)
             one_over_den = work.tile([P, 1], F32, name="one_over_den")
             nc.vector.reciprocal(one_over_den[:], pairs[:, CHANNELS:WITH_ONE])
             scaled = work.tile([P, CHANNELS], F32, name="scaled", bufs=BLOCKS)

@@ -13,7 +13,8 @@ BLOCKS = NODES // P
 WITH_ONE = CHANNELS + 1
 H2_FROM = WITH_ONE + 1
 MOVING_COLS = 2 * H2_FROM
-MOVING_PITCH = MOVING_COLS + 28
+ALIGN = 256
+MOVING_PITCH = 3 * ALIGN // 2
 TILE_COLS = 256
 TILES = NODES // TILE_COLS
 BLOCKS_A_TILE = TILE_COLS // P
@@ -32,12 +33,12 @@ def tile_bgnna_kernel(tc, base, h, et, bias, offs, out):
         tc.tile_pool(name="work", bufs=5) as work,
         tc.psum_pool(name="psum", bufs=2) as psum,
     ):
-        moving = held.tile([P, BLOCKS, MOVING_PITCH], BF16, name="moving")
+        moving = held.tile([P, BLOCKS, MOVING_PITCH], BF16, name="moving", align_bytes=ALIGN)
         nc.vector.memset(moving[:, :, CHANNELS:H2_FROM], 1.0)
         nc.sync.dma_start(moving[:, :, 0:CHANNELS], h.rearrange("(kb p) c -> p kb c", p=P))
 
         et_blocks = et.rearrange("(kb p) j -> p kb j", p=P)
-        a = [held.tile([P, BLOCKS, TILE_COLS], BF16, name=f"a{g}") for g in range(TILES)]
+        a = [held.tile([P, BLOCKS, TILE_COLS], BF16, name=f"a{g}", align_bytes=ALIGN) for g in range(TILES)]
         for g in range(TILES):
             for rows in (slice(0, HALF), slice(HALF, BLOCKS)):
                 queue = nc.scalar if (g == 0 and rows.start == 0) else nc.sync
@@ -47,14 +48,14 @@ def tile_bgnna_kernel(tc, base, h, et, bias, offs, out):
         nc.sync.dma_start(offsets[:], offs)
         bias_col = held.tile([P, 1], F32, name="bias_col")
         nc.gpsimd.dma_start(bias_col[:], bias)
-        bias_wide = held.tile([P, NODES], F32, name="bias_wide")
+        bias_wide = held.tile([P, NODES], F32, name="bias_wide", align_bytes=ALIGN)
         nc.gpsimd.tensor_copy(bias_wide[:], bias_col[:, 0:1].to_broadcast([P, NODES]))
-        window = held.tile([P, SLOTS], F32, name="window")
+        window = held.tile([P, SLOTS], F32, name="window", align_bytes=ALIGN)
         nc.sync.dma_start(window[:], base)
 
-        identity_bf16 = held.tile([P, P], BF16, name="identity_bf16")
+        identity_bf16 = held.tile([P, P], BF16, name="identity_bf16", align_bytes=ALIGN)
         make_identity(nc, identity_bf16[:])
-        identity_f32 = held.tile([P, P], F32, name="identity_f32")
+        identity_f32 = held.tile([P, P], F32, name="identity_f32", align_bytes=ALIGN)
         make_identity(nc, identity_f32[:])
 
         nc.scalar.activation(moving[:, :, MOVING_COLS - 2 : MOVING_COLS], moving[:, :, CHANNELS:H2_FROM], SQUARE)
@@ -62,9 +63,9 @@ def tile_bgnna_kernel(tc, base, h, et, bias, offs, out):
                                 moving[:, 0:HALF, 0:CHANNELS], MULT)
         nc.scalar.activation(moving[:, HALF:BLOCKS, H2_FROM : H2_FROM + CHANNELS], moving[:, HALF:BLOCKS, 0:CHANNELS], SQUARE)
 
-        diagonal = held.tile([P, BLOCKS, P], BF16, name="diagonal")
-        diagonal_squared = held.tile([P, BLOCKS, P], BF16, name="diagonal_squared")
-        values = held.tile([P, NODES], F32, name="values")
+        diagonal = held.tile([P, BLOCKS, P], BF16, name="diagonal", align_bytes=ALIGN)
+        diagonal_squared = held.tile([P, BLOCKS, P], BF16, name="diagonal_squared", align_bytes=ALIGN)
+        values = held.tile([P, NODES], F32, name="values", align_bytes=ALIGN)
 
         def a_block(kb, jb):
             g, r = divmod(jb, BLOCKS_A_TILE)
@@ -91,13 +92,13 @@ def tile_bgnna_kernel(tc, base, h, et, bias, offs, out):
             nc.tensor.matmul(sq_t[:, H2_FROM:MOVING_COLS], diagonal_squared[:, jb, :],
                              moving[:, jb, H2_FROM:MOVING_COLS], start=False, stop=True)
 
-            s_squared = work.tile([P, WITH_ONE], F32, name="s_squared")
+            s_squared = work.tile([P, WITH_ONE], F32, name="s_squared", align_bytes=ALIGN)
             nc.scalar.activation(s_squared[:], sq_t[:, 0:WITH_ONE], SQUARE)
-            pairs = work.tile([P, WITH_ONE], F32, name="pairs")
+            pairs = work.tile([P, WITH_ONE], F32, name="pairs", align_bytes=ALIGN)
             nc.vector.tensor_tensor(pairs[:], s_squared[:], sq_t[:, H2_FROM : H2_FROM + WITH_ONE], SUBTRACT)
             one_over_den = work.tile([P, 1], F32, name="one_over_den")
             nc.vector.reciprocal(one_over_den[:], pairs[:, CHANNELS:WITH_ONE])
-            scaled = work.tile([P, CHANNELS], F32, name="scaled", bufs=BLOCKS)
+            scaled = work.tile([P, CHANNELS], F32, name="scaled", bufs=BLOCKS, align_bytes=ALIGN)
             nc.vector.tensor_scalar(scaled[:], pairs[:, 0:CHANNELS], one_over_den[:], None, MULT)
             scaled_blocks.append(scaled)
 

@@ -2,7 +2,8 @@ import concourse.mybir as mybir
 from concourse.masks import make_identity
 
 BF16, F32, U16 = mybir.dt.bfloat16, mybir.dt.float32, mybir.dt.uint16
-ADD, SUBTRACT, MULT = mybir.AluOpType.add, mybir.AluOpType.subtract, mybir.AluOpType.mult
+ADD, SUBTRACT, MULT, IS_EQUAL = (mybir.AluOpType.add, mybir.AluOpType.subtract, mybir.AluOpType.mult,
+                                 mybir.AluOpType.is_equal)
 SQUARE, COPY = mybir.ActivationFunctionType.Square, mybir.ActivationFunctionType.Copy
 
 P = 128
@@ -41,8 +42,7 @@ def tile_bgnna_kernel(tc, base, h, et, bias, offs, out):
         a = [held.tile([P, BLOCKS, TILE_COLS], BF16, name=f"a{g}", align_bytes=ALIGN) for g in range(TILES)]
         for g in range(TILES):
             for rows in (slice(0, HALF), slice(HALF, BLOCKS)):
-                queue = nc.scalar if (g == 0 and rows.start == 0) else nc.sync
-                queue.dma_start(a[g][:, rows, :], et_blocks[:, rows, g * TILE_COLS : (g + 1) * TILE_COLS])
+                nc.sync.dma_start(a[g][:, rows, :], et_blocks[:, rows, g * TILE_COLS : (g + 1) * TILE_COLS])
 
         offsets = held.tile([P, NODES // 16], U16, name="offsets")
         nc.sync.dma_start(offsets[:], offs)
@@ -53,8 +53,16 @@ def tile_bgnna_kernel(tc, base, h, et, bias, offs, out):
         window = held.tile([P, SLOTS], F32, name="window", align_bytes=ALIGN)
         nc.sync.dma_start(window[:], base)
 
+        ones_f32 = held.tile([P, P], F32, name="ones_f32", align_bytes=ALIGN)
+        nc.vector.memset(ones_f32[:], 1.0)
+        ramp = held.tile([P, P], BF16, name="ramp", align_bytes=ALIGN)
+        nc.vector.tensor_tensor_scan(ramp[:], ones_f32[:], ones_f32[:], -1.0, MULT, ADD)
+        share = held.tile([P, 1], BF16, name="share")
+        nc.vector.memset(share[:], 1.0 / P)
+        own_index = psum.tile([P, 1], F32, name="own_index", tag="turned", bufs=len(TURN_GROUPS))
+        nc.tensor.matmul(own_index[:], ramp[:], share[:], start=True, stop=True)
         identity_bf16 = held.tile([P, P], BF16, name="identity_bf16", align_bytes=ALIGN)
-        make_identity(nc, identity_bf16[:])
+        nc.vector.tensor_scalar(identity_bf16[:], ramp[:], own_index[:, 0:1], None, IS_EQUAL)
         identity_f32 = held.tile([P, P], F32, name="identity_f32", align_bytes=ALIGN)
         make_identity(nc, identity_f32[:])
 

@@ -1,5 +1,4 @@
 import concourse.mybir as mybir
-from concourse.masks import make_identity
 
 BF16, F32, U16 = mybir.dt.bfloat16, mybir.dt.float32, mybir.dt.uint16
 ADD, SUBTRACT, MULT, IS_EQUAL = (mybir.AluOpType.add, mybir.AluOpType.subtract, mybir.AluOpType.mult,
@@ -47,9 +46,9 @@ def tile_bgnna_kernel(tc, base, h, et, bias, offs, out):
         offsets = held.tile([P, NODES // 16], U16, name="offsets")
         nc.sync.dma_start(offsets[:], offs)
         bias_col = held.tile([P, 1], F32, name="bias_col")
-        nc.gpsimd.dma_start(bias_col[:], bias)
+        nc.scalar.dma_start(bias_col[:], bias)
         bias_wide = held.tile([P, NODES], F32, name="bias_wide", align_bytes=ALIGN)
-        nc.gpsimd.tensor_copy(bias_wide[:], bias_col[:, 0:1].to_broadcast([P, NODES]))
+        nc.scalar.activation(bias_wide[:], bias_col[:, 0:1].to_broadcast([P, NODES]), COPY)
         window = held.tile([P, SLOTS], F32, name="window", align_bytes=ALIGN)
         nc.sync.dma_start(window[:], base)
 
@@ -64,7 +63,7 @@ def tile_bgnna_kernel(tc, base, h, et, bias, offs, out):
         identity_bf16 = held.tile([P, P], BF16, name="identity_bf16", align_bytes=ALIGN)
         nc.vector.tensor_scalar(identity_bf16[:], ramp[:], own_index[:, 0:1], None, IS_EQUAL)
         identity_f32 = held.tile([P, P], F32, name="identity_f32", align_bytes=ALIGN)
-        make_identity(nc, identity_f32[:])
+        nc.vector.tensor_scalar(identity_f32[:], ramp[:], own_index[:, 0:1], None, IS_EQUAL)
 
         nc.scalar.activation(moving[:, :, MOVING_COLS - 2 : MOVING_COLS], moving[:, :, CHANNELS:H2_FROM], SQUARE)
         nc.vector.tensor_tensor(moving[:, 0:HALF, H2_FROM : H2_FROM + CHANNELS], moving[:, 0:HALF, 0:CHANNELS],

@@ -35,12 +35,14 @@ def tile_bgnna_kernel(tc, base, h, et, bias, offs, out):
     ):
         moving = held.tile([P, BLOCKS, MOVING_PITCH], BF16, name="moving", align_bytes=ALIGN)
         nc.vector.memset(moving[:, :, CHANNELS:H2_FROM], 1.0)
-        nc.sync.dma_start(moving[:, :, 0:CHANNELS], h.rearrange("(kb p) c -> p kb c", p=P))
+        h_blocks = h.rearrange("(kb p) c -> p kb c", p=P)
 
         et_blocks = et.rearrange("(kb p) j -> p kb j", p=P)
         a = [held.tile([P, BLOCKS, TILE_COLS], BF16, name=f"a{g}", align_bytes=ALIGN) for g in range(TILES)]
         for g in range(TILES):
             for rows in (slice(0, HALF), slice(HALF, BLOCKS)):
+                if g == 0:
+                    nc.sync.dma_start(moving[:, rows, 0:CHANNELS], h_blocks[:, rows, :])
                 nc.sync.dma_start(a[g][:, rows, :], et_blocks[:, rows, g * TILE_COLS : (g + 1) * TILE_COLS])
 
         offsets = held.tile([P, NODES // 16], U16, name="offsets")
@@ -66,9 +68,9 @@ def tile_bgnna_kernel(tc, base, h, et, bias, offs, out):
         nc.vector.tensor_scalar(identity_f32[:], ramp[:], own_index[:, 0:1], None, IS_EQUAL)
 
         nc.scalar.activation(moving[:, :, MOVING_COLS - 2 : MOVING_COLS], moving[:, :, CHANNELS:H2_FROM], SQUARE)
-        nc.vector.tensor_tensor(moving[:, 0:HALF, H2_FROM : H2_FROM + CHANNELS], moving[:, 0:HALF, 0:CHANNELS],
-                                moving[:, 0:HALF, 0:CHANNELS], MULT)
-        nc.scalar.activation(moving[:, HALF:BLOCKS, H2_FROM : H2_FROM + CHANNELS], moving[:, HALF:BLOCKS, 0:CHANNELS], SQUARE)
+        for rows in (slice(0, HALF), slice(HALF, BLOCKS)):
+            nc.vector.tensor_tensor(moving[:, rows, H2_FROM : H2_FROM + CHANNELS], moving[:, rows, 0:CHANNELS],
+                                    moving[:, rows, 0:CHANNELS], MULT)
 
         diagonal = held.tile([P, BLOCKS, P], BF16, name="diagonal", align_bytes=ALIGN)
         diagonal_squared = held.tile([P, BLOCKS, P], BF16, name="diagonal_squared", align_bytes=ALIGN)
@@ -101,12 +103,14 @@ def tile_bgnna_kernel(tc, base, h, et, bias, offs, out):
 
             s_squared = work.tile([P, WITH_ONE], F32, name="s_squared", align_bytes=ALIGN)
             nc.scalar.activation(s_squared[:], sq_t[:, 0:WITH_ONE], SQUARE)
-            pairs = work.tile([P, WITH_ONE], F32, name="pairs", align_bytes=ALIGN)
-            nc.vector.tensor_tensor(pairs[:], s_squared[:], sq_t[:, H2_FROM : H2_FROM + WITH_ONE], SUBTRACT)
+            den = work.tile([P, 1], F32, name="den")
+            nc.vector.tensor_tensor(den[:], s_squared[:, CHANNELS:WITH_ONE], sq_t[:, H2_FROM + CHANNELS : H2_FROM + WITH_ONE], SUBTRACT)
+            pairs = work.tile([P, CHANNELS], F32, name="pairs", align_bytes=ALIGN)
+            nc.vector.tensor_tensor(pairs[:], s_squared[:, 0:CHANNELS], sq_t[:, H2_FROM : H2_FROM + CHANNELS], SUBTRACT)
             one_over_den = work.tile([P, 1], F32, name="one_over_den")
-            nc.vector.reciprocal(one_over_den[:], pairs[:, CHANNELS:WITH_ONE])
+            nc.vector.reciprocal(one_over_den[:], den[:])
             scaled = work.tile([P, CHANNELS], F32, name="scaled", bufs=BLOCKS, align_bytes=ALIGN)
-            nc.vector.tensor_scalar(scaled[:], pairs[:, 0:CHANNELS], one_over_den[:], None, MULT)
+            nc.vector.tensor_scalar(scaled[:], pairs[:], one_over_den[:], None, MULT)
             scaled_blocks.append(scaled)
 
         for group in TURN_GROUPS:

@@ -20,7 +20,8 @@ TILES = NODES // TILE_COLS
 BLOCKS_A_TILE = TILE_COLS // P
 HALF = BLOCKS // 2
 AHEAD = 2
-TURN_GROUPS = ((0, 1, 2, 3), (4, 5, 6), (7,))
+BEHIND = 2
+TURN_BANKS = 3
 STORES = 4
 
 FLOPS = 2 * 2 * WITH_ONE * NODES * NODES
@@ -60,7 +61,7 @@ def tile_bgnna_kernel(tc, base, h, et, bias, offs, out):
         nc.vector.tensor_tensor_scan(ramp[:], ones_f32[:], ones_f32[:], -1.0, MULT, ADD)
         share = held.tile([P, 1], BF16, name="share")
         nc.vector.memset(share[:], 1.0 / P)
-        own_index = psum.tile([P, 1], F32, name="own_index", tag="turned", bufs=len(TURN_GROUPS))
+        own_index = psum.tile([P, 1], F32, name="own_index", tag="turned", bufs=TURN_BANKS)
         nc.tensor.matmul(own_index[:], ramp[:], share[:], start=True, stop=True)
         identity_bf16 = held.tile([P, P], BF16, name="identity_bf16", align_bytes=ALIGN)
         nc.vector.tensor_scalar(identity_bf16[:], ramp[:], own_index[:, 0:1], None, IS_EQUAL)
@@ -83,6 +84,11 @@ def tile_bgnna_kernel(tc, base, h, et, bias, offs, out):
         def prepare(jb):
             nc.vector.tensor_tensor(diagonal[:, jb, :], a_block(jb, jb), identity_bf16[:], ADD)
             nc.scalar.activation(diagonal_squared[:, jb, :], diagonal[:, jb, :], SQUARE)
+
+        def turn(jb):
+            turned = psum.tile([P, P], F32, name="turned", bufs=TURN_BANKS)
+            nc.tensor.transpose(turned[:], scaled_blocks[jb][:], identity_f32[:])
+            nc.scalar.activation(values[:, jb * P : (jb + 1) * P], turned[:], COPY)
 
         scaled_blocks = []
         for jb in range(AHEAD):
@@ -112,16 +118,11 @@ def tile_bgnna_kernel(tc, base, h, et, bias, offs, out):
             scaled = work.tile([P, CHANNELS], F32, name="scaled", bufs=BLOCKS, align_bytes=ALIGN)
             nc.vector.tensor_scalar(scaled[:], pairs[:], one_over_den[:], None, MULT)
             scaled_blocks.append(scaled)
+            if jb >= BEHIND:
+                turn(jb - BEHIND)
 
-        for group in TURN_GROUPS:
-            turned = psum.tile([P, len(group) * P], F32, name="turned", bufs=len(TURN_GROUPS))
-            for i, jb in enumerate(group):
-                nc.tensor.transpose(turned[:, i * P : (i + 1) * P], scaled_blocks[jb][:], identity_f32[:])
-            group_values = values[:, group[0] * P : (group[-1] + 1) * P]
-            if group == TURN_GROUPS[1]:
-                nc.vector.tensor_copy(group_values, turned[:])
-            else:
-                nc.scalar.activation(group_values, turned[:], COPY)
+        for jb in range(BLOCKS - BEHIND, BLOCKS):
+            turn(jb)
 
         nc.vector.tensor_tensor(window[:].indirect(offsets[:]), values[:], bias_wide[:], ADD)
 

@@ -22,6 +22,7 @@ HALF = BLOCKS // 2
 AHEAD = 2
 BEHIND = 2
 TURN_BANKS = 3
+PRODUCT_BANKS = 5
 STORES = 4
 
 FLOPS = 2 * 2 * WITH_ONE * NODES * NODES
@@ -97,22 +98,32 @@ def tile_bgnna_kernel(tc, base, h, et, bias, offs, out):
             if jb + AHEAD < BLOCKS:
                 prepare(jb + AHEAD)
 
-            sq_t = psum.tile([P, MOVING_COLS], F32, name="sq_t", bufs=5)
             others = [(jb + 1 + i) % BLOCKS for i in range(BLOCKS - 1)]
-            for kb in others:
-                nc.tensor.matmul(sq_t[:], a_block(kb, jb), moving[:, kb, 0:MOVING_COLS],
-                                 start=(kb == others[0]), stop=False)
-            nc.tensor.matmul(sq_t[:, 0:H2_FROM], diagonal[:, jb, :], moving[:, jb, 0:H2_FROM],
-                             start=False, stop=False)
-            nc.tensor.matmul(sq_t[:, H2_FROM:MOVING_COLS], diagonal_squared[:, jb, :],
-                             moving[:, jb, H2_FROM:MOVING_COLS], start=False, stop=True)
+            if jb < BLOCKS - 1:
+                sq_t = psum.tile([P, MOVING_COLS], F32, name="sq_t", tag="products", bufs=PRODUCT_BANKS)
+                s_t, q_t = sq_t[:, 0:H2_FROM], sq_t[:, H2_FROM:MOVING_COLS]
+                for kb in others:
+                    nc.tensor.matmul(sq_t[:], a_block(kb, jb), moving[:, kb, 0:MOVING_COLS],
+                                     start=(kb == others[0]), stop=False)
+                nc.tensor.matmul(s_t, diagonal[:, jb, :], moving[:, jb, 0:H2_FROM], start=False, stop=False)
+                nc.tensor.matmul(q_t, diagonal_squared[:, jb, :], moving[:, jb, H2_FROM:MOVING_COLS],
+                                 start=False, stop=True)
+            else:
+                s_t = psum.tile([P, H2_FROM], F32, name="s_t", tag="products", bufs=PRODUCT_BANKS)[:]
+                q_t = psum.tile([P, H2_FROM], F32, name="q_t", tag="products", bufs=PRODUCT_BANKS)[:]
+                for product, first_col, on_diagonal in ((s_t, 0, diagonal), (q_t, H2_FROM, diagonal_squared)):
+                    for kb in others:
+                        nc.tensor.matmul(product, a_block(kb, jb), moving[:, kb, first_col : first_col + H2_FROM],
+                                         start=(kb == others[0]), stop=False)
+                    nc.tensor.matmul(product, on_diagonal[:, jb, :], moving[:, jb, first_col : first_col + H2_FROM],
+                                     start=False, stop=True)
 
             s_squared = work.tile([P, WITH_ONE], F32, name="s_squared", align_bytes=ALIGN)
-            nc.scalar.activation(s_squared[:], sq_t[:, 0:WITH_ONE], SQUARE)
+            nc.scalar.activation(s_squared[:], s_t[:, 0:WITH_ONE], SQUARE)
             den = work.tile([P, 1], F32, name="den")
-            nc.vector.tensor_tensor(den[:], s_squared[:, CHANNELS:WITH_ONE], sq_t[:, H2_FROM + CHANNELS : H2_FROM + WITH_ONE], SUBTRACT)
+            nc.vector.tensor_tensor(den[:], s_squared[:, CHANNELS:WITH_ONE], q_t[:, CHANNELS:WITH_ONE], SUBTRACT)
             pairs = work.tile([P, CHANNELS], F32, name="pairs", align_bytes=ALIGN)
-            nc.vector.tensor_tensor(pairs[:], s_squared[:, 0:CHANNELS], sq_t[:, H2_FROM : H2_FROM + CHANNELS], SUBTRACT)
+            nc.vector.tensor_tensor(pairs[:], s_squared[:, 0:CHANNELS], q_t[:, 0:CHANNELS], SUBTRACT)
             one_over_den = work.tile([P, 1], F32, name="one_over_den")
             nc.vector.reciprocal(one_over_den[:], den[:])
             scaled = work.tile([P, CHANNELS], F32, name="scaled", bufs=BLOCKS, align_bytes=ALIGN)

@@ -89,7 +89,10 @@ def tile_bgnna_kernel(tc, base, h, et, bias, offs, out):
         def turn(jb):
             turned = psum.tile([P, P], F32, name="turned", bufs=TURN_BANKS)
             nc.tensor.transpose(turned[:], scaled_blocks[jb][:], identity_f32[:])
-            nc.scalar.activation(values[:, jb * P : (jb + 1) * P], turned[:], COPY)
+            if jb % 2 == 0:
+                nc.vector.tensor_copy(values[:, jb * P : (jb + 1) * P], turned[:])
+            else:
+                nc.scalar.activation(values[:, jb * P : (jb + 1) * P], turned[:], COPY)
 
         scaled_blocks = []
         for jb in range(AHEAD):

import concourse.mybir as mybir

BF16, F32, U16 = mybir.dt.bfloat16, mybir.dt.float32, mybir.dt.uint16
ADD, SUBTRACT, MULT, IS_EQUAL = (mybir.AluOpType.add, mybir.AluOpType.subtract, mybir.AluOpType.mult,
                                 mybir.AluOpType.is_equal)
SQUARE, COPY = mybir.ActivationFunctionType.Square, mybir.ActivationFunctionType.Copy

P = 128
CHANNELS = 128
SLOTS = 4096
NODES = 1024
BLOCKS = NODES // P
WITH_ONE = CHANNELS + 1
H2_FROM = WITH_ONE + 1
MOVING_COLS = 2 * H2_FROM
ALIGN = 256
MOVING_PITCH = 3 * ALIGN // 2
TILE_COLS = 256
TILES = NODES // TILE_COLS
BLOCKS_A_TILE = TILE_COLS // P
HALF = BLOCKS // 2
AHEAD = 2
BEHIND = 2
TURN_BANKS = 3
PRODUCT_BANKS = 5
STORES = 4

FLOPS = 2 * 2 * WITH_ONE * NODES * NODES


def tile_bgnna_kernel(tc, base, h, et, bias, offs, out):
    nc = tc.nc
    with (
        tc.tile_pool(name="held", bufs=1) as held,
        tc.tile_pool(name="work", bufs=5) as work,
        tc.psum_pool(name="psum", bufs=2) as psum,
    ):
        moving = held.tile([P, BLOCKS, MOVING_PITCH], BF16, name="moving", align_bytes=ALIGN)
        nc.vector.memset(moving[:, :, CHANNELS:H2_FROM], 1.0)
        h_blocks = h.rearrange("(kb p) c -> p kb c", p=P)

        et_blocks = et.rearrange("(kb p) j -> p kb j", p=P)
        a = [held.tile([P, BLOCKS, TILE_COLS], BF16, name=f"a{g}", align_bytes=ALIGN) for g in range(TILES)]
        for g in range(TILES):
            for rows in (slice(0, HALF), slice(HALF, BLOCKS)):
                if g == 0:
                    nc.sync.dma_start(moving[:, rows, 0:CHANNELS], h_blocks[:, rows, :])
                nc.sync.dma_start(a[g][:, rows, :], et_blocks[:, rows, g * TILE_COLS : (g + 1) * TILE_COLS])

        offsets = held.tile([P, NODES // 16], U16, name="offsets")
        nc.sync.dma_start(offsets[:], offs)
        bias_col = held.tile([P, 1], F32, name="bias_col")
        nc.scalar.dma_start(bias_col[:], bias)
        bias_wide = held.tile([P, NODES], F32, name="bias_wide", align_bytes=ALIGN)
        nc.scalar.activation(bias_wide[:], bias_col[:, 0:1].to_broadcast([P, NODES]), COPY)
        window = held.tile([P, SLOTS], F32, name="window", align_bytes=ALIGN)
        nc.sync.dma_start(window[:], base)

        ones_f32 = held.tile([P, P], F32, name="ones_f32", align_bytes=ALIGN)
        nc.vector.memset(ones_f32[:], 1.0)
        ramp = held.tile([P, P], BF16, name="ramp", align_bytes=ALIGN)
        nc.vector.tensor_tensor_scan(ramp[:], ones_f32[:], ones_f32[:], -1.0, MULT, ADD)
        share = held.tile([P, 1], BF16, name="share")
        nc.vector.memset(share[:], 1.0 / P)
        own_index = psum.tile([P, 1], F32, name="own_index", tag="turned", bufs=TURN_BANKS)
        nc.tensor.matmul(own_index[:], ramp[:], share[:], start=True, stop=True)
        identity_bf16 = held.tile([P, P], BF16, name="identity_bf16", align_bytes=ALIGN)
        nc.vector.tensor_scalar(identity_bf16[:], ramp[:], own_index[:, 0:1], None, IS_EQUAL)
        identity_f32 = held.tile([P, P], F32, name="identity_f32", align_bytes=ALIGN)
        nc.vector.tensor_scalar(identity_f32[:], ramp[:], own_index[:, 0:1], None, IS_EQUAL)

        nc.scalar.activation(moving[:, :, MOVING_COLS - 2 : MOVING_COLS], moving[:, :, CHANNELS:H2_FROM], SQUARE)
        for rows in (slice(0, HALF), slice(HALF, BLOCKS)):
            nc.vector.tensor_tensor(moving[:, rows, H2_FROM : H2_FROM + CHANNELS], moving[:, rows, 0:CHANNELS],
                                    moving[:, rows, 0:CHANNELS], MULT)

        diagonal = held.tile([P, BLOCKS, P], BF16, name="diagonal", align_bytes=ALIGN)
        diagonal_squared = held.tile([P, BLOCKS, P], BF16, name="diagonal_squared", align_bytes=ALIGN)
        values = held.tile([P, NODES], F32, name="values", align_bytes=ALIGN)

        def a_block(kb, jb):
            g, r = divmod(jb, BLOCKS_A_TILE)
            return a[g][:, kb, r * P : (r + 1) * P]

        def prepare(jb):
            nc.vector.tensor_tensor(diagonal[:, jb, :], a_block(jb, jb), identity_bf16[:], ADD)
            nc.scalar.activation(diagonal_squared[:, jb, :], diagonal[:, jb, :], SQUARE)

        def turn(jb):
            turned = psum.tile([P, P], F32, name="turned", bufs=TURN_BANKS)
            nc.tensor.transpose(turned[:], scaled_blocks[jb][:], identity_f32[:])
            if jb % 2 == 0:
                nc.vector.tensor_copy(values[:, jb * P : (jb + 1) * P], turned[:])
            else:
                nc.scalar.activation(values[:, jb * P : (jb + 1) * P], turned[:], COPY)

        scaled_blocks = []
        for jb in range(AHEAD):
            prepare(jb)
        for jb in range(BLOCKS):
            if jb + AHEAD < BLOCKS:
                prepare(jb + AHEAD)

            others = [(jb + 1 + i) % BLOCKS for i in range(BLOCKS - 1)]
            if jb < BLOCKS - 1:
                sq_t = psum.tile([P, MOVING_COLS], F32, name="sq_t", tag="products", bufs=PRODUCT_BANKS)
                s_t, q_t = sq_t[:, 0:H2_FROM], sq_t[:, H2_FROM:MOVING_COLS]
                for kb in others:
                    nc.tensor.matmul(sq_t[:], a_block(kb, jb), moving[:, kb, 0:MOVING_COLS],
                                     start=(kb == others[0]), stop=False)
                nc.tensor.matmul(s_t, diagonal[:, jb, :], moving[:, jb, 0:H2_FROM], start=False, stop=False)
                nc.tensor.matmul(q_t, diagonal_squared[:, jb, :], moving[:, jb, H2_FROM:MOVING_COLS],
                                 start=False, stop=True)
            else:
                s_t = psum.tile([P, H2_FROM], F32, name="s_t", tag="products", bufs=PRODUCT_BANKS)[:]
                q_t = psum.tile([P, H2_FROM], F32, name="q_t", tag="products", bufs=PRODUCT_BANKS)[:]
                for product, first_col, on_diagonal in ((s_t, 0, diagonal), (q_t, H2_FROM, diagonal_squared)):
                    for kb in others:
                        nc.tensor.matmul(product, a_block(kb, jb), moving[:, kb, first_col : first_col + H2_FROM],
                                         start=(kb == others[0]), stop=False)
                    nc.tensor.matmul(product, on_diagonal[:, jb, :], moving[:, jb, first_col : first_col + H2_FROM],
                                     start=False, stop=True)

            s_squared = work.tile([P, WITH_ONE], F32, name="s_squared", align_bytes=ALIGN)
            nc.scalar.activation(s_squared[:], s_t[:, 0:WITH_ONE], SQUARE)
            den = work.tile([P, 1], F32, name="den")
            nc.vector.tensor_tensor(den[:], s_squared[:, CHANNELS:WITH_ONE], q_t[:, CHANNELS:WITH_ONE], SUBTRACT)
            pairs = work.tile([P, CHANNELS], F32, name="pairs", align_bytes=ALIGN)
            nc.vector.tensor_tensor(pairs[:], s_squared[:, 0:CHANNELS], q_t[:, 0:CHANNELS], SUBTRACT)
            one_over_den = work.tile([P, 1], F32, name="one_over_den")
            nc.vector.reciprocal(one_over_den[:], den[:])
            scaled = work.tile([P, CHANNELS], F32, name="scaled", bufs=BLOCKS, align_bytes=ALIGN)
            nc.vector.tensor_scalar(scaled[:], pairs[:], one_over_den[:], None, MULT)
            scaled_blocks.append(scaled)
            if jb >= BEHIND:
                turn(jb - BEHIND)

        for jb in range(BLOCKS - BEHIND, BLOCKS):
            turn(jb)

        nc.vector.tensor_tensor(window[:].indirect(offsets[:]), values[:], bias_wide[:], ADD)

        width = SLOTS // STORES
        for piece in range(STORES):
            queue = nc.sync if piece % 2 == 0 else nc.scalar
            queue.dma_start(out[:, piece * width : (piece + 1) * width],
                            window[:, piece * width : (piece + 1) * width])
